import numpy as np
import ml_dtypes


def mxq(x, axis, fmt="e4m3"):
    dtype, down = {"e4m3": (ml_dtypes.float8_e4m3fn, 7), "e5m2": (ml_dtypes.float8_e5m2, 14)}[fmt]
    v = np.moveaxis(np.asarray(x, np.float32).astype(ml_dtypes.bfloat16).astype(np.float64), axis, -1)
    blocks = v.reshape(v.shape[:-1] + (-1, 32))
    amax = np.abs(blocks).max(-1, keepdims=True)
    byte = np.maximum(np.where(amax > 0, np.frexp(amax)[1] - 1 + 127, 0) - down, 1)
    scale = np.exp2(byte - 127.0)
    codes = (blocks / scale).astype(np.float32).astype(dtype).astype(np.float64)
    return np.moveaxis((codes * scale).reshape(v.shape), -1, axis)


WIDE = False


def mx_kscale(k):
    if not WIDE:
        return np.ones(k)
    levels = np.array([10, -10, 5, -5, 0])
    a = np.random.permutation(np.resize(levels, k // 512 * 4)).reshape(k // 512, 4)
    idx = np.arange(k)
    return np.exp2(a[idx // 512, idx % 128 // 32])


BF16 = ml_dtypes.bfloat16


def bf(x):
    return np.asarray(x, np.float32).astype(BF16)


def f64(x):
    return np.asarray(x).astype(np.float64)


N, L, WD, C, O = 128, 64, 512, 512, 512
EPS = 1e-8
CONV_CLAMP = 256.0
ACT_GAIN = np.sqrt(2.0)
LRELU_SLOPE = 0.2
STYLE_WSCALE = 1.0 / np.sqrt(WD)
X_AMP = CONV_CLAMP / 2.0
W_AMP = np.sqrt(EPS)


def setup_inputs():
    s, t = mx_kscale(WD), mx_kscale(C)
    return {"x": bf(np.random.standard_normal((N, L, C)) * X_AMP),
            "w": bf(np.random.standard_normal((N, WD)) * s),
            "weight": bf(np.random.standard_normal((O, C)) * W_AMP / np.sqrt(C) / t[None, :]),
            "style_w": bf(np.random.standard_normal((C, WD)) * t[:, None] / s[None, :]),
            "style_b": bf((1.0 + 0.1 * np.random.standard_normal(C)) * t),
            "bias": bf(np.random.standard_normal(O) * 0.2 * X_AMP)}


def reference(x, w, weight, style_w, style_b, bias):
    wt = f64(weight)
    style = (mxq(f64(w), 1, "e4m3") @ mxq(f64(style_w), 1, "e4m3").T) * STYLE_WSCALE + f64(style_b)
    d = mxq(np.square(style), 1, "e4m3") @ mxq(np.square(wt), 1, "e4m3").T
    decoef = 1.0 / np.sqrt(d + EPS)
    x_mod = f64(x) * style[:, None, :]
    y = mxq(x_mod, 2, "e4m3") @ mxq(wt, 1, "e4m3").T
    y = y * decoef[:, None, :]
    y = y + f64(bias)
    y = np.where(y >= 0, y, LRELU_SLOPE * y) * ACT_GAIN
    return np.clip(y, -CONV_CLAMP, CONV_CLAMP)

@@ -1,0 +1,254 @@
+import math
+
+import concourse.mybir as mybir
+from concourse.masks import make_identity
+
+F32 = mybir.dt.float32
+BF16 = mybir.dt.bfloat16
+U32 = mybir.dt.uint32
+U8 = mybir.dt.uint8
+FP8X4 = mybir.dt.float8_e4m3fn_x4
+ALU = mybir.AluOpType
+ACT = mybir.ActivationFunctionType
+
+P = 128
+PACK = 4
+HALVES = 2
+SAMPLES, POINTS, WIDTH = 128, 64, 512
+CHUNKS = WIDTH // P
+TOKENS = SAMPLES * POINTS
+GROUP = 512
+GROUPS = TOKENS // GROUP
+TILES = GROUP // P
+BANK_ROWS = 2 * P
+BANK_SAMPLES = BANK_ROWS // POINTS
+GROUP_SAMPLES = GROUP // POINTS
+
+EPS = 1e-8
+CLAMP = 256.0
+SLOPE = 0.2
+GAIN_SQUARED = 2.0
+GAIN = math.sqrt(GAIN_SQUARED)
+STYLE_WSCALE = 1.0 / math.sqrt(WIDTH)
+
+FLOPS = 2 * TOKENS * WIDTH * WIDTH + 2 * 2 * SAMPLES * WIDTH * WIDTH
+
+
+def transpose_row_tiles(nc, bank, words, ident):
+    for s in range(words.shape[1]):
+        for u in range(HALVES):
+            nc.tensor.transpose(
+                bank[:, u, s * P : (s + 1) * P], words[:, s, u * P : (u + 1) * P], ident[:]
+            )
+
+
+def quantise(nc, pool, grouped, name):
+    columns = grouped.shape[1]
+    codes = pool.tile([P, columns], U32, align_bytes=64, name=name + "_codes")
+    scales = pool.tile([P, columns], U8, align_bytes=64, name=name + "_scales")
+    nc.vector.quantize_mx(
+        out=codes[:].bitcast(FP8X4),
+        scales=scales[:],
+        in_=grouped[:].rearrange("p r t -> p (r t)"),
+    )
+    return codes, scales
+
+
+def multiply_mx(nc, acc, stationary, first_column, moving):
+    cols = slice(first_column, first_column + P)
+    nc.tensor.matmul_mx(
+        out=acc,
+        lhsT=stationary[0][:, cols].bitcast(FP8X4),
+        lhsT_scale=stationary[1][:, cols],
+        rhs=moving[0][:].bitcast(FP8X4),
+        rhs_scale=moving[1][:],
+        start=True,
+        stop=True,
+    )
+
+
+def tile_modulatemlp_pa_kernel(tc, x, w, weight, style_w, style_b, bias, out):
+    nc = tc.nc
+    x_rows = x.rearrange("n l c -> (n l) c")
+    out_rows = out.rearrange("n l o -> (n l) o")
+
+    with tc.tile_pool(name="const", bufs=1) as const, tc.tile_pool(
+        name="xin", bufs=GROUPS
+    ) as xin, tc.tile_pool(name="xq", bufs=2) as xq, tc.tile_pool(
+        name="mid", bufs=3
+    ) as mid, tc.tile_pool(name="fin", bufs=4) as fin, tc.psum_pool(name="psum", bufs=1) as psum:
+        ident = const.tile([P, P], F32)
+        make_identity(nc, ident[:])
+
+        sb_bf = const.tile([P, PACK], BF16)
+        bias_bf = const.tile([P, CHUNKS], BF16)
+        with nc.allow_non_contiguous_dma(reason="two small vectors, one or two elements a piece"):
+            nc.sync.dma_start(
+                out=sb_bf[:].rearrange("p (u e) -> p u e", e=2),
+                in_=style_b.rearrange("(u p e) -> p u e", u=HALVES, e=2),
+            )
+            nc.scalar.dma_start(out=bias_bf[:], in_=bias.rearrange("(j p) -> p j", p=P))
+        w_sb = const.tile([P, 1, WIDTH], BF16)
+        nc.sync.dma_start(out=w_sb[:, 0, :], in_=w)
+        sw_sb = const.tile([P, PACK, WIDTH], BF16)
+        nc.sync.dma_start(
+            out=sw_sb[:].rearrange("p (u e) k -> p u (e k)", e=2),
+            in_=style_w.rearrange("(u p e) k -> p u (e k)", u=HALVES, e=2),
+        )
+        wt_sb = const.tile([P, CHUNKS, WIDTH], BF16)
+        nc.sync.dma_start(out=wt_sb[:], in_=weight.rearrange("(j p) c -> p j c", p=P))
+        x_tiles = []
+        for g in range(GROUPS):
+            x_sb = xin.tile([P, TILES, WIDTH], BF16)
+            nc.sync.dma_start(
+                out=x_sb[:],
+                in_=x_rows[g * GROUP : (g + 1) * GROUP, :].rearrange("(t p) c -> p t c", p=P),
+            )
+            x_tiles.append(x_sb)
+
+        w_bank = psum.tile([P, HALVES, P], F32, tag="xT0")
+        transpose_row_tiles(nc, w_bank, w_sb[:].bitcast(F32), ident)
+        w_grp = const.tile([P, SAMPLES, PACK], BF16, align_bytes=64)
+        nc.vector.tensor_copy(out=w_grp[:].bitcast(F32), in_=w_bank[:].rearrange("p u r -> p r u"))
+
+        sw_grp = const.tile([P, WIDTH, PACK], BF16, align_bytes=64)
+        for h, tag in enumerate(("xT1", "oT0")):
+            sw_bank = psum.tile([P, HALVES, BANK_ROWS], F32, tag=tag)
+            transpose_row_tiles(nc, sw_bank, sw_sb[:].bitcast(F32)[:, 2 * h : 2 * h + 2, :], ident)
+            nc.vector.tensor_copy(
+                out=sw_grp[:].bitcast(F32)[:, h * BANK_ROWS : (h + 1) * BANK_ROWS, :],
+                in_=sw_bank[:].rearrange("p u r -> p r u"),
+            )
+        w_q = quantise(nc, const, w_grp, "w")
+        sw_q = quantise(nc, const, sw_grp, "sw")
+
+        style_ps = psum.tile([P, PACK, SAMPLES], F32, tag="y0")
+        for t in range(PACK):
+            multiply_mx(nc, style_ps[:, t, :], sw_q, t * P, w_q)
+        style4 = const.tile([P, SAMPLES, PACK], F32)
+        nc.vector.scalar_tensor_tensor(
+            out=style4[:],
+            in0=style_ps[:].rearrange("p t n -> p n t"),
+            scalar=STYLE_WSCALE,
+            in1=sb_bf[:].unsqueeze(1).to_broadcast([P, SAMPLES, PACK]),
+            op0=ALU.mult,
+            op1=ALU.add,
+        )
+
+        wt_grp = const.tile([P, WIDTH, PACK], BF16, align_bytes=64)
+        w2_grp = const.tile([P, WIDTH, PACK], BF16, align_bytes=64)
+        for h, tag in enumerate(("oT1", "y3")):
+            wt_bank = psum.tile([P, HALVES, BANK_ROWS], F32, tag=tag)
+            rows = slice(h * BANK_ROWS, (h + 1) * BANK_ROWS)
+            transpose_row_tiles(nc, wt_bank, wt_sb[:].bitcast(F32)[:, 2 * h : 2 * h + 2, :], ident)
+            nc.scalar.copy(
+                out=wt_grp[:].bitcast(F32)[:, rows, :], in_=wt_bank[:].rearrange("p u r -> p r u")
+            )
+            nc.scalar.activation(
+                out=w2_grp[:, rows, :].rearrange("p r (u e) -> p r u e", e=2),
+                in_=wt_bank[:].bitcast(BF16).rearrange("p u (r e) -> p r u e", e=2),
+                func=ACT.Square,
+            )
+        wt_q = quantise(nc, const, wt_grp, "wt")
+        w2_q = quantise(nc, const, w2_grp, "w2")
+
+        s2_grp = const.tile([P, SAMPLES, PACK], BF16, align_bytes=64)
+        nc.scalar.activation(out=s2_grp[:], in_=style4[:], func=ACT.Square)
+        s2_q = quantise(nc, const, s2_grp, "s2")
+        d_ps = psum.tile([P, CHUNKS, SAMPLES], F32, tag="y1")
+        for j in range(CHUNKS):
+            multiply_mx(nc, d_ps[:, j, :], w2_q, j * P, s2_q)
+        root = const.tile([P, CHUNKS, SAMPLES], F32)
+        nc.scalar.activation(
+            out=root[:], in_=d_ps[:], func=ACT.Sqrt, scale=1.0 / GAIN_SQUARED, bias=EPS / GAIN_SQUARED
+        )
+        demod = const.tile([P, CHUNKS, SAMPLES], F32)
+        nc.vector.reciprocal(out=demod[:], in_=root[:])
+        bias_g = const.tile([P, CHUNKS], F32)
+        nc.vector.tensor_scalar(
+            out=bias_g[:], in0=bias_bf[:], scalar1=GAIN, scalar2=None, op0=ALU.mult
+        )
+
+        grouped = {}
+        x_q = {}
+        y_banks = {}
+        u_tiles = {}
+
+        def modulate(g, h):
+            if h == 0:
+                x_grp = xq.tile([P, GROUP, PACK], BF16, align_bytes=64)
+                grouped[g] = x_grp
+            bank = psum.tile([P, HALVES, BANK_ROWS], F32, tag="xT%d" % h)
+            transpose_row_tiles(
+                nc, bank, x_tiles[g][:].bitcast(F32)[:, 2 * h : 2 * h + 2, :], ident
+            )
+            first = g * GROUP_SAMPLES + h * BANK_SAMPLES
+            nc.vector.tensor_tensor(
+                out=grouped[g][:, h * BANK_ROWS : (h + 1) * BANK_ROWS, :].rearrange(
+                    "p (n l) (u e) -> p n l u e", l=POINTS, e=2
+                ),
+                in0=bank[:].bitcast(BF16).rearrange("p u (n l e) -> p n l u e", l=POINTS, e=2),
+                in1=style4[:, first : first + BANK_SAMPLES, :]
+                .rearrange("p n (u e) -> p n u e", e=2)
+                .unsqueeze(2)
+                .to_broadcast([P, BANK_SAMPLES, POINTS, HALVES, 2]),
+                op=ALU.mult,
+            )
+
+        def multiply(g):
+            y_banks[g] = []
+            for j in range(CHUNKS):
+                y = psum.tile([P, GROUP], F32, tag="y%d" % j)
+                multiply_mx(nc, y[:], wt_q, j * P, x_q[g])
+                y_banks[g].append(y)
+
+        def demodulate(g, j):
+            if j == 0:
+                u = mid.tile([P, CHUNKS, GROUP], F32)
+                u_tiles[g] = u
+            for s in range(GROUP_SAMPLES):
+                n = g * GROUP_SAMPLES + s
+                cols = slice(s * POINTS, (s + 1) * POINTS)
+                nc.scalar.activation(
+                    out=u_tiles[g][:, j, cols],
+                    in_=y_banks[g][j][:, cols],
+                    func=ACT.Identity,
+                    scale=demod[:, j, n : n + 1],
+                    bias=bias_g[:, j : j + 1],
+                )
+            nc.gpsimd.tensor_scalar(
+                out=u_tiles[g][:, j, :],
+                in0=u_tiles[g][:, j, :],
+                scalar1=CLAMP,
+                scalar2=-CLAMP / SLOPE,
+                op0=ALU.min,
+                op1=ALU.max,
+            )
+
+        def finish(g, t):
+            o_bank = psum.tile([P, WIDTH], F32, tag="oT%d" % (t % 2))
+            for j in range(CHUNKS):
+                nc.tensor.transpose(
+                    o_bank[:, j * P : (j + 1) * P], u_tiles[g][:, j, t * P : (t + 1) * P], ident[:]
+                )
+            pos = fin.tile([P, WIDTH], F32)
+            nc.scalar.activation(out=pos[:], in_=o_bank[:], func=ACT.Relu, scale=1.0 - SLOPE)
+            res = fin.tile([P, WIDTH], F32)
+            nc.vector.scalar_tensor_tensor(
+                out=res[:], in0=o_bank[:], scalar=SLOPE, in1=pos[:], op0=ALU.mult, op1=ALU.add
+            )
+            first = g * GROUP + t * P
+            nc.sync.dma_start(out=out_rows[first : first + P, :], in_=res[:])
+
+        for step in range(GROUPS + 2):
+            if 0 <= step - 1 < GROUPS:
+                multiply(step - 1)
+            for q in range(TILES):
+                if 0 <= step - 1 < GROUPS:
+                    demodulate(step - 1, q)
+                if 0 <= step - 2 < GROUPS:
+                    finish(step - 2, q)
+                if step < GROUPS and q < 2:
+                    modulate(step, q)
+                if step < GROUPS and q == 2:
+                    x_q[step] = quantise(nc, xq, grouped[step], "x")

@@ -216,9 +216,11 @@ def tile_modulatemlp_pa_kernel(tc, x, w, weight, style_w, style_b, bias, out):
                     scale=demod[:, j, n : n + 1],
                     bias=bias_g[:, j : j + 1],
                 )
-            nc.gpsimd.tensor_scalar(
-                out=u_tiles[g][:, j, :],
-                in0=u_tiles[g][:, j, :],
+
+        def clamp(g):
+            nc.vector.tensor_scalar(
+                out=u_tiles[g][:],
+                in0=u_tiles[g][:],
                 scalar1=CLAMP,
                 scalar2=-CLAMP / SLOPE,
                 op0=ALU.min,
@@ -252,3 +254,5 @@ def tile_modulatemlp_pa_kernel(tc, x, w, weight, style_w, style_b, bias, out):
                     modulate(step, q)
                 if step < GROUPS and q == 2:
                     x_q[step] = quantise(nc, xq, grouped[step], "x")
+            if 0 <= step - 1 < GROUPS:
+                clamp(step - 1)

@@ -217,10 +217,11 @@ def tile_modulatemlp_pa_kernel(tc, x, w, weight, style_w, style_b, bias, out):
                     bias=bias_g[:, j : j + 1],
                 )
 
-        def clamp(g):
-            nc.vector.tensor_scalar(
-                out=u_tiles[g][:],
-                in0=u_tiles[g][:],
+        def clamp(engine, g, first_chunk):
+            half = u_tiles[g][:, first_chunk : first_chunk + CHUNKS // 2, :]
+            engine.tensor_scalar(
+                out=half,
+                in0=half,
                 scalar1=CLAMP,
                 scalar2=-CLAMP / SLOPE,
                 op0=ALU.min,
@@ -254,5 +255,7 @@ def tile_modulatemlp_pa_kernel(tc, x, w, weight, style_w, style_b, bias, out):
                     modulate(step, q)
                 if step < GROUPS and q == 2:
                     x_q[step] = quantise(nc, xq, grouped[step], "x")
+                if 0 <= step - 1 < GROUPS and q == 1:
+                    clamp(nc.gpsimd, step - 1, 0)
             if 0 <= step - 1 < GROUPS:
-                clamp(step - 1)
+                clamp(nc.vector, step - 1, CHUNKS // 2)

@@ -27,8 +27,9 @@ GROUP_SAMPLES = GROUP // POINTS
 EPS = 1e-8
 CLAMP = 256.0
 SLOPE = 0.2
-GAIN_SQUARED = 2.0
-GAIN = math.sqrt(GAIN_SQUARED)
+GAIN = math.sqrt(2.0)
+LOW_GAIN = GAIN * SLOPE
+LOW_GAIN_SQUARED = 2.0 * SLOPE * SLOPE
 STYLE_WSCALE = 1.0 / math.sqrt(WIDTH)
 
 FLOPS = 2 * TOKENS * WIDTH * WIDTH + 2 * 2 * SAMPLES * WIDTH * WIDTH
@@ -160,19 +161,20 @@ def tile_modulatemlp_pa_kernel(tc, x, w, weight, style_w, style_b, bias, out):
             multiply_mx(nc, d_ps[:, j, :], w2_q, j * P, s2_q)
         root = const.tile([P, CHUNKS, SAMPLES], F32)
         nc.scalar.activation(
-            out=root[:], in_=d_ps[:], func=ACT.Sqrt, scale=1.0 / GAIN_SQUARED, bias=EPS / GAIN_SQUARED
+            out=root[:], in_=d_ps[:], func=ACT.Sqrt, scale=1.0 / LOW_GAIN_SQUARED, bias=EPS / LOW_GAIN_SQUARED
         )
         demod = const.tile([P, CHUNKS, SAMPLES], F32)
         nc.vector.reciprocal(out=demod[:], in_=root[:])
         bias_g = const.tile([P, CHUNKS], F32)
         nc.vector.tensor_scalar(
-            out=bias_g[:], in0=bias_bf[:], scalar1=GAIN, scalar2=None, op0=ALU.mult
+            out=bias_g[:], in0=bias_bf[:], scalar1=LOW_GAIN, scalar2=None, op0=ALU.mult
         )
 
         grouped = {}
         x_q = {}
         y_banks = {}
-        u_tiles = {}
+        low_tiles = {}
+        rest_tiles = {}
 
         def modulate(g, h):
             if h == 0:
@@ -204,41 +206,49 @@ def tile_modulatemlp_pa_kernel(tc, x, w, weight, style_w, style_b, bias, out):
 
         def demodulate(g, j):
             if j == 0:
-                u = mid.tile([P, CHUNKS, GROUP], F32)
-                u_tiles[g] = u
+                low = mid.tile([P, CHUNKS, GROUP], F32)
+                low_tiles[g] = low
             for s in range(GROUP_SAMPLES):
                 n = g * GROUP_SAMPLES + s
                 cols = slice(s * POINTS, (s + 1) * POINTS)
                 nc.scalar.activation(
-                    out=u_tiles[g][:, j, cols],
+                    out=low_tiles[g][:, j, cols],
                     in_=y_banks[g][j][:, cols],
                     func=ACT.Identity,
                     scale=demod[:, j, n : n + 1],
                     bias=bias_g[:, j : j + 1],
                 )
 
-        def clamp(engine, g, first_chunk):
-            half = u_tiles[g][:, first_chunk : first_chunk + CHUNKS // 2, :]
-            engine.tensor_scalar(
-                out=half,
-                in0=half,
-                scalar1=CLAMP,
-                scalar2=-CLAMP / SLOPE,
-                op0=ALU.min,
-                op1=ALU.max,
+        def rectify(g, first_chunk):
+            if first_chunk == 0:
+                rest = mid.tile([P, CHUNKS, GROUP], F32)
+                rest_tiles[g] = rest
+            half = slice(first_chunk, first_chunk + CHUNKS // 2)
+            nc.gpsimd.tensor_scalar(
+                out=rest_tiles[g][:, half, :],
+                in0=low_tiles[g][:, half, :],
+                scalar1=0.0,
+                scalar2=1.0 / SLOPE - 1.0,
+                op0=ALU.max,
+                op1=ALU.mult,
             )
 
         def finish(g, t):
             o_bank = psum.tile([P, WIDTH], F32, tag="oT%d" % (t % 2))
+            tokens = slice(t * P, (t + 1) * P)
             for j in range(CHUNKS):
-                nc.tensor.transpose(
-                    o_bank[:, j * P : (j + 1) * P], u_tiles[g][:, j, t * P : (t + 1) * P], ident[:]
-                )
-            pos = fin.tile([P, WIDTH], F32)
-            nc.scalar.activation(out=pos[:], in_=o_bank[:], func=ACT.Relu, scale=1.0 - SLOPE)
+                for part in (low_tiles[g], rest_tiles[g]):
+                    nc.tensor.matmul(
+                        o_bank[:, j * P : (j + 1) * P],
+                        lhsT=part[:, j, tokens],
+                        rhs=ident[:],
+                        start=part is low_tiles[g],
+                        stop=part is rest_tiles[g],
+                        is_transpose=True,
+                    )
             res = fin.tile([P, WIDTH], F32)
-            nc.vector.scalar_tensor_tensor(
-                out=res[:], in0=o_bank[:], scalar=SLOPE, in1=pos[:], op0=ALU.mult, op1=ALU.add
+            nc.vector.tensor_scalar(
+                out=res[:], in0=o_bank[:], scalar1=CLAMP, scalar2=-CLAMP, op0=ALU.min, op1=ALU.max
             )
             first = g * GROUP + t * P
             nc.sync.dma_start(out=out_rows[first : first + P, :], in_=res[:])
@@ -255,7 +265,5 @@ def tile_modulatemlp_pa_kernel(tc, x, w, weight, style_w, style_b, bias, out):
                     modulate(step, q)
                 if step < GROUPS and q == 2:
                     x_q[step] = quantise(nc, xq, grouped[step], "x")
-                if 0 <= step - 1 < GROUPS and q == 1:
-                    clamp(nc.gpsimd, step - 1, 0)
-            if 0 <= step - 1 < GROUPS:
-                clamp(nc.vector, step - 1, CHUNKS // 2)
+                if 0 <= step - 1 < GROUPS and q % 2 == 1:
+                    rectify(step - 1, q - 1)

@@ -24,6 +24,11 @@ BANK_ROWS = 2 * P
 BANK_SAMPLES = BANK_ROWS // POINTS
 GROUP_SAMPLES = GROUP // POINTS
 
+SCALAR_TILES = (1, 3)
+
+Y_BANKS = 3
+O_BANKS = 3
+
 EPS = 1e-8
 CLAMP = 256.0
 SLOPE = 0.2
@@ -75,9 +80,9 @@ def tile_modulatemlp_pa_kernel(tc, x, w, weight, style_w, style_b, bias, out):
 
     with tc.tile_pool(name="const", bufs=1) as const, tc.tile_pool(
         name="xin", bufs=GROUPS
-    ) as xin, tc.tile_pool(name="xq", bufs=2) as xq, tc.tile_pool(
-        name="mid", bufs=3
-    ) as mid, tc.tile_pool(name="fin", bufs=4) as fin, tc.psum_pool(name="psum", bufs=1) as psum:
+    ) as xin, tc.tile_pool(name="xq", bufs=3) as xq, tc.tile_pool(
+        name="mid", bufs=4
+    ) as mid, tc.tile_pool(name="fin", bufs=6) as fin, tc.psum_pool(name="psum", bufs=1) as psum, tc.manual_schedule():
         ident = const.tile([P, P], F32)
         make_identity(nc, ident[:])
 
@@ -107,13 +112,13 @@ def tile_modulatemlp_pa_kernel(tc, x, w, weight, style_w, style_b, bias, out):
             )
             x_tiles.append(x_sb)
 
-        w_bank = psum.tile([P, HALVES, P], F32, tag="xT0")
+        w_bank = psum.tile([P, HALVES, P], F32, tag="o0")
         transpose_row_tiles(nc, w_bank, w_sb[:].bitcast(F32), ident)
         w_grp = const.tile([P, SAMPLES, PACK], BF16, align_bytes=64)
         nc.vector.tensor_copy(out=w_grp[:].bitcast(F32), in_=w_bank[:].rearrange("p u r -> p r u"))
 
         sw_grp = const.tile([P, WIDTH, PACK], BF16, align_bytes=64)
-        for h, tag in enumerate(("xT1", "oT0")):
+        for h, tag in enumerate(("o1", "o2")):
             sw_bank = psum.tile([P, HALVES, BANK_ROWS], F32, tag=tag)
             transpose_row_tiles(nc, sw_bank, sw_sb[:].bitcast(F32)[:, 2 * h : 2 * h + 2, :], ident)
             nc.vector.tensor_copy(
@@ -123,73 +128,54 @@ def tile_modulatemlp_pa_kernel(tc, x, w, weight, style_w, style_b, bias, out):
         w_q = quantise(nc, const, w_grp, "w")
         sw_q = quantise(nc, const, sw_grp, "sw")
 
-        style_ps = psum.tile([P, PACK, SAMPLES], F32, tag="y0")
-        for t in range(PACK):
-            multiply_mx(nc, style_ps[:, t, :], sw_q, t * P, w_q)
-        style4 = const.tile([P, SAMPLES, PACK], F32)
-        nc.vector.scalar_tensor_tensor(
-            out=style4[:],
-            in0=style_ps[:].rearrange("p t n -> p n t"),
-            scalar=STYLE_WSCALE,
-            in1=sb_bf[:].unsqueeze(1).to_broadcast([P, SAMPLES, PACK]),
-            op0=ALU.mult,
-            op1=ALU.add,
-        )
-
         wt_grp = const.tile([P, WIDTH, PACK], BF16, align_bytes=64)
         w2_grp = const.tile([P, WIDTH, PACK], BF16, align_bytes=64)
-        for h, tag in enumerate(("oT1", "y3")):
+        for h, tag in enumerate(("y1", "y2")):
             wt_bank = psum.tile([P, HALVES, BANK_ROWS], F32, tag=tag)
             rows = slice(h * BANK_ROWS, (h + 1) * BANK_ROWS)
             transpose_row_tiles(nc, wt_bank, wt_sb[:].bitcast(F32)[:, 2 * h : 2 * h + 2, :], ident)
-            nc.scalar.copy(
-                out=wt_grp[:].bitcast(F32)[:, rows, :], in_=wt_bank[:].rearrange("p u r -> p r u")
-            )
             nc.scalar.activation(
                 out=w2_grp[:, rows, :].rearrange("p r (u e) -> p r u e", e=2),
                 in_=wt_bank[:].bitcast(BF16).rearrange("p u (r e) -> p r u e", e=2),
                 func=ACT.Square,
             )
-        wt_q = quantise(nc, const, wt_grp, "wt")
-        w2_q = quantise(nc, const, w2_grp, "w2")
-
-        s2_grp = const.tile([P, SAMPLES, PACK], BF16, align_bytes=64)
-        nc.scalar.activation(out=s2_grp[:], in_=style4[:], func=ACT.Square)
-        s2_q = quantise(nc, const, s2_grp, "s2")
-        d_ps = psum.tile([P, CHUNKS, SAMPLES], F32, tag="y1")
-        for j in range(CHUNKS):
-            multiply_mx(nc, d_ps[:, j, :], w2_q, j * P, s2_q)
-        root = const.tile([P, CHUNKS, SAMPLES], F32)
-        nc.scalar.activation(
-            out=root[:], in_=d_ps[:], func=ACT.Sqrt, scale=1.0 / LOW_GAIN_SQUARED, bias=EPS / LOW_GAIN_SQUARED
-        )
-        demod = const.tile([P, CHUNKS, SAMPLES], F32)
-        nc.vector.reciprocal(out=demod[:], in_=root[:])
+            nc.scalar.copy(
+                out=wt_grp[:].bitcast(F32)[:, rows, :], in_=wt_bank[:].rearrange("p u r -> p r u")
+            )
         bias_g = const.tile([P, CHUNKS], F32)
         nc.vector.tensor_scalar(
             out=bias_g[:], in0=bias_bf[:], scalar1=LOW_GAIN, scalar2=None, op0=ALU.mult
         )
 
+        style4 = const.tile([P, SAMPLES, PACK], F32)
+        demod = const.tile([P, CHUNKS, SAMPLES], F32)
+        x_banks = {}
         grouped = {}
         x_q = {}
         y_banks = {}
         low_tiles = {}
         rest_tiles = {}
+        o_banks = {}
+
+        def transpose_in(g, h):
+            bank = psum.tile([P, HALVES, BANK_ROWS], F32, tag="xT%d" % h)
+            transpose_row_tiles(
+                nc, bank, x_tiles[g][:].bitcast(F32)[:, 2 * h : 2 * h + 2, :], ident
+            )
+            x_banks[g, h] = bank
 
         def modulate(g, h):
             if h == 0:
                 x_grp = xq.tile([P, GROUP, PACK], BF16, align_bytes=64)
                 grouped[g] = x_grp
-            bank = psum.tile([P, HALVES, BANK_ROWS], F32, tag="xT%d" % h)
-            transpose_row_tiles(
-                nc, bank, x_tiles[g][:].bitcast(F32)[:, 2 * h : 2 * h + 2, :], ident
-            )
             first = g * GROUP_SAMPLES + h * BANK_SAMPLES
             nc.vector.tensor_tensor(
                 out=grouped[g][:, h * BANK_ROWS : (h + 1) * BANK_ROWS, :].rearrange(
                     "p (n l) (u e) -> p n l u e", l=POINTS, e=2
                 ),
-                in0=bank[:].bitcast(BF16).rearrange("p u (n l e) -> p n l u e", l=POINTS, e=2),
+                in0=x_banks[g, h][:]
+                .bitcast(BF16)
+                .rearrange("p u (n l e) -> p n l u e", l=POINTS, e=2),
                 in1=style4[:, first : first + BANK_SAMPLES, :]
                 .rearrange("p n (u e) -> p n u e", e=2)
                 .unsqueeze(2)
@@ -197,12 +183,10 @@ def tile_modulatemlp_pa_kernel(tc, x, w, weight, style_w, style_b, bias, out):
                 op=ALU.mult,
             )
 
-        def multiply(g):
-            y_banks[g] = []
-            for j in range(CHUNKS):
-                y = psum.tile([P, GROUP], F32, tag="y%d" % j)
-                multiply_mx(nc, y[:], wt_q, j * P, x_q[g])
-                y_banks[g].append(y)
+        def multiply(g, j):
+            y = psum.tile([P, GROUP], F32, tag="y%d" % ((g * CHUNKS + j) % Y_BANKS))
+            multiply_mx(nc, y[:], wt_q, j * P, x_q[g])
+            y_banks[g, j] = y
 
         def demodulate(g, j):
             if j == 0:
@@ -213,57 +197,111 @@ def tile_modulatemlp_pa_kernel(tc, x, w, weight, style_w, style_b, bias, out):
                 cols = slice(s * POINTS, (s + 1) * POINTS)
                 nc.scalar.activation(
                     out=low_tiles[g][:, j, cols],
-                    in_=y_banks[g][j][:, cols],
+                    in_=y_banks[g, j][:, cols],
                     func=ACT.Identity,
                     scale=demod[:, j, n : n + 1],
                     bias=bias_g[:, j : j + 1],
                 )
 
-        def rectify(g, first_chunk):
-            if first_chunk == 0:
+        def clamp(g, half):
+            chunks = low_tiles[g][:, 2 * half : 2 * half + 2, :]
+            nc.gpsimd.tensor_scalar(
+                out=chunks,
+                in0=chunks,
+                scalar1=SLOPE * CLAMP,
+                scalar2=-CLAMP,
+                op0=ALU.min,
+                op1=ALU.max,
+            )
+
+        def rectify(g, half):
+            if half == 0:
                 rest = mid.tile([P, CHUNKS, GROUP], F32)
                 rest_tiles[g] = rest
-            half = slice(first_chunk, first_chunk + CHUNKS // 2)
-            nc.gpsimd.tensor_scalar(
-                out=rest_tiles[g][:, half, :],
-                in0=low_tiles[g][:, half, :],
+            chunks = slice(2 * half, 2 * half + 2)
+            nc.vector.tensor_scalar(
+                out=rest_tiles[g][:, chunks, :],
+                in0=low_tiles[g][:, chunks, :],
                 scalar1=0.0,
                 scalar2=1.0 / SLOPE - 1.0,
                 op0=ALU.max,
                 op1=ALU.mult,
             )
 
-        def finish(g, t):
-            o_bank = psum.tile([P, WIDTH], F32, tag="oT%d" % (t % 2))
+        def transpose_out(g, t):
+            bank = psum.tile([P, WIDTH], F32, tag="o%d" % ((g * TILES + t) % O_BANKS))
             tokens = slice(t * P, (t + 1) * P)
             for j in range(CHUNKS):
                 for part in (low_tiles[g], rest_tiles[g]):
                     nc.tensor.matmul(
-                        o_bank[:, j * P : (j + 1) * P],
+                        bank[:, j * P : (j + 1) * P],
                         lhsT=part[:, j, tokens],
                         rhs=ident[:],
                         start=part is low_tiles[g],
                         stop=part is rest_tiles[g],
                         is_transpose=True,
                     )
+            o_banks[g, t] = bank
+
+        def store(g, t):
             res = fin.tile([P, WIDTH], F32)
-            nc.vector.tensor_scalar(
-                out=res[:], in0=o_bank[:], scalar1=CLAMP, scalar2=-CLAMP, op0=ALU.min, op1=ALU.max
-            )
+            if t in SCALAR_TILES:
+                nc.scalar.copy(out=res[:], in_=o_banks[g, t][:])
+            else:
+                nc.vector.tensor_copy(out=res[:], in_=o_banks[g, t][:])
             first = g * GROUP + t * P
             nc.sync.dma_start(out=out_rows[first : first + P, :], in_=res[:])
 
-        for step in range(GROUPS + 2):
-            if 0 <= step - 1 < GROUPS:
-                multiply(step - 1)
-            for q in range(TILES):
-                if 0 <= step - 1 < GROUPS:
-                    demodulate(step - 1, q)
-                if 0 <= step - 2 < GROUPS:
-                    finish(step - 2, q)
-                if step < GROUPS and q < 2:
-                    modulate(step, q)
-                if step < GROUPS and q == 2:
-                    x_q[step] = quantise(nc, xq, grouped[step], "x")
-                if 0 <= step - 1 < GROUPS and q % 2 == 1:
-                    rectify(step - 1, q - 1)
+        transpose_in(0, 0)
+        transpose_in(0, 1)
+
+        style_ps = psum.tile([P, PACK, SAMPLES], F32, tag="y0")
+        for t in range(PACK):
+            multiply_mx(nc, style_ps[:, t, :], sw_q, t * P, w_q)
+        nc.vector.scalar_tensor_tensor(
+            out=style4[:],
+            in0=style_ps[:].rearrange("p t n -> p n t"),
+            scalar=STYLE_WSCALE,
+            in1=sb_bf[:].unsqueeze(1).to_broadcast([P, SAMPLES, PACK]),
+            op0=ALU.mult,
+            op1=ALU.add,
+        )
+        s2_grp = const.tile([P, SAMPLES, PACK], BF16, align_bytes=64)
+        nc.scalar.activation(out=s2_grp[:], in_=style4[:], func=ACT.Square)
+        modulate(0, 0)
+        w2_q = quantise(nc, const, w2_grp, "w2")
+        s2_q = quantise(nc, const, s2_grp, "s2")
+        modulate(0, 1)
+        wt_q = quantise(nc, const, wt_grp, "wt")
+
+        d_ps = psum.tile([P, CHUNKS, SAMPLES], F32, tag="y1")
+        for j in range(CHUNKS):
+            multiply_mx(nc, d_ps[:, j, :], w2_q, j * P, s2_q)
+        nc.scalar.activation(
+            out=demod[:],
+            in_=d_ps[:],
+            func=ACT.Abs_reciprocal_sqrt,
+            scale=1.0 / LOW_GAIN_SQUARED,
+            bias=EPS / LOW_GAIN_SQUARED,
+        )
+
+        for step in range(GROUPS + 5):
+            if 0 <= step - 2 < GROUPS:
+                x_q[step - 2] = quantise(nc, xq, grouped[step - 2], "x")
+            for q in range(4):
+                if 0 <= step - 5 < GROUPS:
+                    transpose_out(step - 5, q)
+                if 0 <= step - 3 < GROUPS:
+                    multiply(step - 3, q)
+                    demodulate(step - 3, q)
+                    if q % 2 == 1:
+                        clamp(step - 3, q // 2)
+                if q % 2 == 0:
+                    if 1 <= step - 1 < GROUPS:
+                        modulate(step - 1, q // 2)
+                    if 1 <= step < GROUPS:
+                        transpose_in(step, q // 2)
+                elif 0 <= step - 4 < GROUPS:
+                    rectify(step - 4, q // 2)
+                if 0 <= step - 5 < GROUPS:
+                    store(step - 5, q)

@@ -26,8 +26,8 @@ GROUP_SAMPLES = GROUP // POINTS
 
 SCALAR_TILES = (1, 3)
 
-Y_BANKS = 3
-O_BANKS = 3
+Y_BANKS = 4
+O_BANKS = 2
 
 EPS = 1e-8
 CLAMP = 256.0
@@ -81,7 +81,7 @@ def tile_modulatemlp_pa_kernel(tc, x, w, weight, style_w, style_b, bias, out):
     with tc.tile_pool(name="const", bufs=1) as const, tc.tile_pool(
         name="xin", bufs=GROUPS
     ) as xin, tc.tile_pool(name="xq", bufs=3) as xq, tc.tile_pool(
-        name="mid", bufs=4
+        name="mid", bufs=5
     ) as mid, tc.tile_pool(name="fin", bufs=6) as fin, tc.psum_pool(name="psum", bufs=1) as psum, tc.manual_schedule():
         ident = const.tile([P, P], F32)
         make_identity(nc, ident[:])
@@ -118,7 +118,7 @@ def tile_modulatemlp_pa_kernel(tc, x, w, weight, style_w, style_b, bias, out):
         nc.vector.tensor_copy(out=w_grp[:].bitcast(F32), in_=w_bank[:].rearrange("p u r -> p r u"))
 
         sw_grp = const.tile([P, WIDTH, PACK], BF16, align_bytes=64)
-        for h, tag in enumerate(("o1", "o2")):
+        for h, tag in enumerate(("o1", "y3")):
             sw_bank = psum.tile([P, HALVES, BANK_ROWS], F32, tag=tag)
             transpose_row_tiles(nc, sw_bank, sw_sb[:].bitcast(F32)[:, 2 * h : 2 * h + 2, :], ident)
             nc.vector.tensor_copy(
@@ -288,20 +288,24 @@ def tile_modulatemlp_pa_kernel(tc, x, w, weight, style_w, style_b, bias, out):
         for step in range(GROUPS + 5):
             if 0 <= step - 2 < GROUPS:
                 x_q[step - 2] = quantise(nc, xq, grouped[step - 2], "x")
-            for q in range(4):
-                if 0 <= step - 5 < GROUPS:
-                    transpose_out(step - 5, q)
+            for h in range(2):
+                pair = (2 * h, 2 * h + 1)
                 if 0 <= step - 3 < GROUPS:
-                    multiply(step - 3, q)
-                    demodulate(step - 3, q)
-                    if q % 2 == 1:
-                        clamp(step - 3, q // 2)
-                if q % 2 == 0:
-                    if 1 <= step - 1 < GROUPS:
-                        modulate(step - 1, q // 2)
-                    if 1 <= step < GROUPS:
-                        transpose_in(step, q // 2)
-                elif 0 <= step - 4 < GROUPS:
-                    rectify(step - 4, q // 2)
+                    for j in pair:
+                        multiply(step - 3, j)
                 if 0 <= step - 5 < GROUPS:
-                    store(step - 5, q)
+                    for t in pair:
+                        transpose_out(step - 5, t)
+                if 1 <= step - 1 < GROUPS:
+                    modulate(step - 1, h)
+                if 1 <= step < GROUPS:
+                    transpose_in(step, h)
+                for q in pair:
+                    if 0 <= step - 3 < GROUPS:
+                        demodulate(step - 3, q)
+                    if 0 <= step - 5 < GROUPS:
+                        store(step - 5, pair[1] if q == pair[0] else pair[0])
+                if 0 <= step - 3 < GROUPS:
+                    clamp(step - 3, h)
+                if 0 <= step - 4 < GROUPS:
+                    rectify(step - 4, h)

@@ -24,7 +24,8 @@ BANK_ROWS = 2 * P
 BANK_SAMPLES = BANK_ROWS // POINTS
 GROUP_SAMPLES = GROUP // POINTS
 
-SCALAR_TILES = (1, 3)
+GPSIMD_CHUNKS = slice(0, 2)
+SCALAR_CHUNKS = slice(2, 4)
 
 Y_BANKS = 4
 O_BANKS = 2
@@ -203,29 +204,33 @@ def tile_modulatemlp_pa_kernel(tc, x, w, weight, style_w, style_b, bias, out):
                     bias=bias_g[:, j : j + 1],
                 )
 
-        def clamp(g, half):
-            chunks = low_tiles[g][:, 2 * half : 2 * half + 2, :]
+        def rectify_gpsimd(g):
+            rest = mid.tile([P, CHUNKS, GROUP], F32)
+            rest_tiles[g] = rest
+            part = rest[:, GPSIMD_CHUNKS, :]
             nc.gpsimd.tensor_scalar(
-                out=chunks,
-                in0=chunks,
+                out=part,
+                in0=low_tiles[g][:, GPSIMD_CHUNKS, :],
                 scalar1=SLOPE * CLAMP,
-                scalar2=-CLAMP,
+                scalar2=0.0,
                 op0=ALU.min,
                 op1=ALU.max,
             )
+            nc.gpsimd.tensor_scalar(
+                out=part,
+                in0=part,
+                scalar1=1.0 / SLOPE - 1.0,
+                scalar2=0.0,
+                op0=ALU.mult,
+                op1=ALU.add,
+            )
 
-        def rectify(g, half):
-            if half == 0:
-                rest = mid.tile([P, CHUNKS, GROUP], F32)
-                rest_tiles[g] = rest
-            chunks = slice(2 * half, 2 * half + 2)
-            nc.vector.tensor_scalar(
-                out=rest_tiles[g][:, chunks, :],
-                in0=low_tiles[g][:, chunks, :],
-                scalar1=0.0,
-                scalar2=1.0 / SLOPE - 1.0,
-                op0=ALU.max,
-                op1=ALU.mult,
+        def rectify_scalar(g):
+            nc.scalar.activation(
+                out=rest_tiles[g][:, SCALAR_CHUNKS, :],
+                in_=low_tiles[g][:, SCALAR_CHUNKS, :],
+                func=ACT.Relu,
+                scale=1.0 / SLOPE - 1.0,
             )
 
         def transpose_out(g, t):
@@ -245,10 +250,14 @@ def tile_modulatemlp_pa_kernel(tc, x, w, weight, style_w, style_b, bias, out):
 
         def store(g, t):
             res = fin.tile([P, WIDTH], F32)
-            if t in SCALAR_TILES:
-                nc.scalar.copy(out=res[:], in_=o_banks[g, t][:])
-            else:
-                nc.vector.tensor_copy(out=res[:], in_=o_banks[g, t][:])
+            nc.vector.tensor_scalar(
+                out=res[:],
+                in0=o_banks[g, t][:],
+                scalar1=CLAMP,
+                scalar2=-CLAMP,
+                op0=ALU.min,
+                op1=ALU.max,
+            )
             first = g * GROUP + t * P
             nc.sync.dma_start(out=out_rows[first : first + P, :], in_=res[:])
 
@@ -300,12 +309,13 @@ def tile_modulatemlp_pa_kernel(tc, x, w, weight, style_w, style_b, bias, out):
                     modulate(step - 1, h)
                 if 1 <= step < GROUPS:
                     transpose_in(step, h)
-                for q in pair:
-                    if 0 <= step - 3 < GROUPS:
-                        demodulate(step - 3, q)
-                    if 0 <= step - 5 < GROUPS:
-                        store(step - 5, pair[1] if q == pair[0] else pair[0])
                 if 0 <= step - 3 < GROUPS:
-                    clamp(step - 3, h)
-                if 0 <= step - 4 < GROUPS:
-                    rectify(step - 4, h)
+                    for j in pair:
+                        demodulate(step - 3, j)
+                if h == 0 and 0 <= step - 3 < GROUPS:
+                    rectify_gpsimd(step - 3)
+                if h == 0 and 0 <= step - 4 < GROUPS:
+                    rectify_scalar(step - 4)
+                if 0 <= step - 5 < GROUPS:
+                    for t in pair:
+                        store(step - 5, t)

@@ -24,11 +24,10 @@ BANK_ROWS = 2 * P
 BANK_SAMPLES = BANK_ROWS // POINTS
 GROUP_SAMPLES = GROUP // POINTS
 
-GPSIMD_CHUNKS = slice(0, 2)
-SCALAR_CHUNKS = slice(2, 4)
+SUMMED_TILE = 3
 
-Y_BANKS = 4
-O_BANKS = 2
+Y_BANKS = 3
+O_BANKS = 3
 
 EPS = 1e-8
 CLAMP = 256.0
@@ -87,23 +86,26 @@ def tile_modulatemlp_pa_kernel(tc, x, w, weight, style_w, style_b, bias, out):
         ident = const.tile([P, P], F32)
         make_identity(nc, ident[:])
 
-        sb_bf = const.tile([P, PACK], BF16)
-        bias_bf = const.tile([P, CHUNKS], BF16)
-        with nc.allow_non_contiguous_dma(reason="two small vectors, one or two elements a piece"):
-            nc.sync.dma_start(
-                out=sb_bf[:].rearrange("p (u e) -> p u e", e=2),
-                in_=style_b.rearrange("(u p e) -> p u e", u=HALVES, e=2),
-            )
-            nc.scalar.dma_start(out=bias_bf[:], in_=bias.rearrange("(j p) -> p j", p=P))
+        style_b_rows = const.tile([P, P], F32)
+        nc.vector.memset(style_b_rows[:], 0.0)
+        bias_rows = const.tile([P, P], F32)
+        nc.vector.memset(bias_rows[:], 0.0)
+        bias_bf = const.tile([CHUNKS, P], BF16)
         w_sb = const.tile([P, 1, WIDTH], BF16)
         nc.sync.dma_start(out=w_sb[:, 0, :], in_=w)
         sw_sb = const.tile([P, PACK, WIDTH], BF16)
-        nc.sync.dma_start(
-            out=sw_sb[:].rearrange("p (u e) k -> p u (e k)", e=2),
-            in_=style_w.rearrange("(u p e) k -> p u (e k)", u=HALVES, e=2),
-        )
+        sw_halves = style_w.rearrange("(u p e) k -> u p (e k)", u=HALVES, e=2)
+        for u in range(HALVES):
+            nc.sync.dma_start(
+                out=sw_sb[:, 2 * u : 2 * u + 2, :].rearrange("p e k -> p (e k)"), in_=sw_halves[u]
+            )
         wt_sb = const.tile([P, CHUNKS, WIDTH], BF16)
         nc.sync.dma_start(out=wt_sb[:], in_=weight.rearrange("(j p) c -> p j c", p=P))
+        nc.sync.dma_start(
+            out=style_b_rows[:HALVES, :].bitcast(BF16),
+            in_=style_b.rearrange("(u q) -> u q", u=HALVES),
+        )
+        nc.sync.dma_start(out=bias_bf[:], in_=bias.rearrange("(j p) -> j p", p=P))
         x_tiles = []
         for g in range(GROUPS):
             x_sb = xin.tile([P, TILES, WIDTH], BF16)
@@ -119,7 +121,7 @@ def tile_modulatemlp_pa_kernel(tc, x, w, weight, style_w, style_b, bias, out):
         nc.vector.tensor_copy(out=w_grp[:].bitcast(F32), in_=w_bank[:].rearrange("p u r -> p r u"))
 
         sw_grp = const.tile([P, WIDTH, PACK], BF16, align_bytes=64)
-        for h, tag in enumerate(("o1", "y3")):
+        for h, tag in enumerate(("o1", "o2")):
             sw_bank = psum.tile([P, HALVES, BANK_ROWS], F32, tag=tag)
             transpose_row_tiles(nc, sw_bank, sw_sb[:].bitcast(F32)[:, 2 * h : 2 * h + 2, :], ident)
             nc.vector.tensor_copy(
@@ -143,9 +145,15 @@ def tile_modulatemlp_pa_kernel(tc, x, w, weight, style_w, style_b, bias, out):
             nc.scalar.copy(
                 out=wt_grp[:].bitcast(F32)[:, rows, :], in_=wt_bank[:].rearrange("p u r -> p r u")
             )
+        nc.vector.tensor_copy(out=bias_rows[:CHUNKS, :], in_=bias_bf[:])
+        vec_bank = psum.tile([P, 2, P], F32, tag="y0")
+        nc.tensor.transpose(vec_bank[:, 0, :], style_b_rows[:], ident[:])
+        nc.tensor.transpose(vec_bank[:, 1, :], bias_rows[:], ident[:])
+        style_b_words = const.tile([P, HALVES], F32)
+        nc.vector.tensor_copy(out=style_b_words[:], in_=vec_bank[:, 0, :HALVES])
         bias_g = const.tile([P, CHUNKS], F32)
         nc.vector.tensor_scalar(
-            out=bias_g[:], in0=bias_bf[:], scalar1=LOW_GAIN, scalar2=None, op0=ALU.mult
+            out=bias_g[:], in0=vec_bank[:, 1, :CHUNKS], scalar1=LOW_GAIN, scalar2=None, op0=ALU.mult
         )
 
         style4 = const.tile([P, SAMPLES, PACK], F32)
@@ -156,6 +164,7 @@ def tile_modulatemlp_pa_kernel(tc, x, w, weight, style_w, style_b, bias, out):
         y_banks = {}
         low_tiles = {}
         rest_tiles = {}
+        pos_tiles = {}
         o_banks = {}
 
         def transpose_in(g, h):
@@ -204,60 +213,80 @@ def tile_modulatemlp_pa_kernel(tc, x, w, weight, style_w, style_b, bias, out):
                     bias=bias_g[:, j : j + 1],
                 )
 
-        def rectify_gpsimd(g):
-            rest = mid.tile([P, CHUNKS, GROUP], F32)
-            rest_tiles[g] = rest
-            part = rest[:, GPSIMD_CHUNKS, :]
+        def clamp(g, j):
+            part = low_tiles[g][:, j, : SUMMED_TILE * P]
             nc.gpsimd.tensor_scalar(
                 out=part,
-                in0=low_tiles[g][:, GPSIMD_CHUNKS, :],
+                in0=part,
+                scalar1=SLOPE * CLAMP,
+                scalar2=-CLAMP,
+                op0=ALU.min,
+                op1=ALU.max,
+            )
+
+        def rectify(g):
+            rest = fin.tile([P, CHUNKS, P], F32)
+            nc.gpsimd.tensor_scalar(
+                out=rest[:],
+                in0=low_tiles[g][:, :, SUMMED_TILE * P : (SUMMED_TILE + 1) * P],
                 scalar1=SLOPE * CLAMP,
                 scalar2=0.0,
                 op0=ALU.min,
                 op1=ALU.max,
             )
             nc.gpsimd.tensor_scalar(
-                out=part,
-                in0=part,
+                out=rest[:],
+                in0=rest[:],
                 scalar1=1.0 / SLOPE - 1.0,
                 scalar2=0.0,
                 op0=ALU.mult,
                 op1=ALU.add,
             )
-
-        def rectify_scalar(g):
-            nc.scalar.activation(
-                out=rest_tiles[g][:, SCALAR_CHUNKS, :],
-                in_=low_tiles[g][:, SCALAR_CHUNKS, :],
-                func=ACT.Relu,
-                scale=1.0 / SLOPE - 1.0,
-            )
+            rest_tiles[g] = rest
 
         def transpose_out(g, t):
             bank = psum.tile([P, WIDTH], F32, tag="o%d" % ((g * TILES + t) % O_BANKS))
-            tokens = slice(t * P, (t + 1) * P)
             for j in range(CHUNKS):
-                for part in (low_tiles[g], rest_tiles[g]):
+                columns = slice(j * P, (j + 1) * P)
+                low = low_tiles[g][:, j, t * P : (t + 1) * P]
+                if t == SUMMED_TILE:
                     nc.tensor.matmul(
-                        bank[:, j * P : (j + 1) * P],
-                        lhsT=part[:, j, tokens],
+                        bank[:, columns], lhsT=low, rhs=ident[:], start=True, stop=False, is_transpose=True
+                    )
+                    nc.tensor.matmul(
+                        bank[:, columns],
+                        lhsT=rest_tiles[g][:, j, :],
                         rhs=ident[:],
-                        start=part is low_tiles[g],
-                        stop=part is rest_tiles[g],
+                        start=False,
+                        stop=True,
                         is_transpose=True,
                     )
+                else:
+                    nc.tensor.transpose(bank[:, columns], low, ident[:])
             o_banks[g, t] = bank
+
+        def rectify_out(g, t):
+            pos = fin.tile([P, WIDTH], F32)
+            nc.scalar.activation(
+                out=pos[:], in_=o_banks[g, t][:], func=ACT.Relu, scale=1.0 / SLOPE - 1.0
+            )
+            pos_tiles[g, t] = pos
 
         def store(g, t):
             res = fin.tile([P, WIDTH], F32)
-            nc.vector.tensor_scalar(
-                out=res[:],
-                in0=o_banks[g, t][:],
-                scalar1=CLAMP,
-                scalar2=-CLAMP,
-                op0=ALU.min,
-                op1=ALU.max,
-            )
+            if t == SUMMED_TILE:
+                nc.vector.tensor_scalar(
+                    out=res[:],
+                    in0=o_banks[g, t][:],
+                    scalar1=CLAMP,
+                    scalar2=-CLAMP,
+                    op0=ALU.min,
+                    op1=ALU.max,
+                )
+            else:
+                nc.vector.tensor_tensor(
+                    out=res[:], in0=o_banks[g, t][:], in1=pos_tiles[g, t][:], op=ALU.add
+                )
             first = g * GROUP + t * P
             nc.sync.dma_start(out=out_rows[first : first + P, :], in_=res[:])
 
@@ -271,17 +300,19 @@ def tile_modulatemlp_pa_kernel(tc, x, w, weight, style_w, style_b, bias, out):
             out=style4[:],
             in0=style_ps[:].rearrange("p t n -> p n t"),
             scalar=STYLE_WSCALE,
-            in1=sb_bf[:].unsqueeze(1).to_broadcast([P, SAMPLES, PACK]),
+            in1=style_b_words[:].bitcast(BF16).unsqueeze(1).to_broadcast([P, SAMPLES, PACK]),
             op0=ALU.mult,
             op1=ALU.add,
         )
         s2_grp = const.tile([P, SAMPLES, PACK], BF16, align_bytes=64)
         nc.scalar.activation(out=s2_grp[:], in_=style4[:], func=ACT.Square)
         modulate(0, 0)
+        transpose_in(1, 0)
         w2_q = quantise(nc, const, w2_grp, "w2")
         s2_q = quantise(nc, const, s2_grp, "s2")
         modulate(0, 1)
         wt_q = quantise(nc, const, wt_grp, "wt")
+        x_q[0] = quantise(nc, xq, grouped[0], "x")
 
         d_ps = psum.tile([P, CHUNKS, SAMPLES], F32, tag="y1")
         for j in range(CHUNKS):
@@ -294,28 +325,36 @@ def tile_modulatemlp_pa_kernel(tc, x, w, weight, style_w, style_b, bias, out):
             bias=EPS / LOW_GAIN_SQUARED,
         )
 
-        for step in range(GROUPS + 5):
-            if 0 <= step - 2 < GROUPS:
+        transpose_in(1, 1)
+        for j in range(CHUNKS):
+            multiply(0, j)
+            demodulate(0, j)
+            clamp(0, j)
+        rectify(0)
+
+        for step in range(2, GROUPS + 5):
+            if 1 <= step - 2 < GROUPS:
                 x_q[step - 2] = quantise(nc, xq, grouped[step - 2], "x")
             for h in range(2):
                 pair = (2 * h, 2 * h + 1)
-                if 0 <= step - 3 < GROUPS:
-                    for j in pair:
-                        multiply(step - 3, j)
                 if 0 <= step - 5 < GROUPS:
                     for t in pair:
                         transpose_out(step - 5, t)
-                if 1 <= step - 1 < GROUPS:
-                    modulate(step - 1, h)
-                if 1 <= step < GROUPS:
-                    transpose_in(step, h)
-                if 0 <= step - 3 < GROUPS:
+                if 1 <= step - 3 < GROUPS:
                     for j in pair:
-                        demodulate(step - 3, j)
-                if h == 0 and 0 <= step - 3 < GROUPS:
-                    rectify_gpsimd(step - 3)
-                if h == 0 and 0 <= step - 4 < GROUPS:
-                    rectify_scalar(step - 4)
+                        multiply(step - 3, j)
+                if step - 1 < GROUPS:
+                    modulate(step - 1, h)
+                if step < GROUPS:
+                    transpose_in(step, h)
+                for q in pair:
+                    if 0 <= step - 5 < GROUPS and q != SUMMED_TILE:
+                        rectify_out(step - 5, q)
+                    if 1 <= step - 3 < GROUPS:
+                        demodulate(step - 3, q)
+                        clamp(step - 3, q)
                 if 0 <= step - 5 < GROUPS:
                     for t in pair:
                         store(step - 5, t)
+                if h == 1 and 1 <= step - 3 < GROUPS:
+                    rectify(step - 3)

@@ -164,7 +164,6 @@ def tile_modulatemlp_pa_kernel(tc, x, w, weight, style_w, style_b, bias, out):
         y_banks = {}
         low_tiles = {}
         rest_tiles = {}
-        pos_tiles = {}
         o_banks = {}
 
         def transpose_in(g, h):
@@ -214,7 +213,7 @@ def tile_modulatemlp_pa_kernel(tc, x, w, weight, style_w, style_b, bias, out):
                 )
 
         def clamp(g, j):
-            part = low_tiles[g][:, j, : SUMMED_TILE * P]
+            part = low_tiles[g][:, j, :]
             nc.gpsimd.tensor_scalar(
                 out=part,
                 in0=part,
@@ -265,27 +264,17 @@ def tile_modulatemlp_pa_kernel(tc, x, w, weight, style_w, style_b, bias, out):
                     nc.tensor.transpose(bank[:, columns], low, ident[:])
             o_banks[g, t] = bank
 
-        def rectify_out(g, t):
-            pos = fin.tile([P, WIDTH], F32)
-            nc.scalar.activation(
-                out=pos[:], in_=o_banks[g, t][:], func=ACT.Relu, scale=1.0 / SLOPE - 1.0
-            )
-            pos_tiles[g, t] = pos
-
-        def store(g, t):
+        def read_out(g, t):
             res = fin.tile([P, WIDTH], F32)
             if t == SUMMED_TILE:
-                nc.vector.tensor_scalar(
-                    out=res[:],
-                    in0=o_banks[g, t][:],
-                    scalar1=CLAMP,
-                    scalar2=-CLAMP,
-                    op0=ALU.min,
-                    op1=ALU.max,
-                )
+                nc.scalar.copy(out=res[:], in_=o_banks[g, t][:])
             else:
+                pos = fin.tile([P, WIDTH], F32)
+                nc.scalar.activation(
+                    out=pos[:], in_=o_banks[g, t][:], func=ACT.Relu, scale=1.0 / SLOPE - 1.0
+                )
                 nc.vector.tensor_tensor(
-                    out=res[:], in0=o_banks[g, t][:], in1=pos_tiles[g, t][:], op=ALU.add
+                    out=res[:], in0=o_banks[g, t][:], in1=pos[:], op=ALU.add
                 )
             first = g * GROUP + t * P
             nc.sync.dma_start(out=out_rows[first : first + P, :], in_=res[:])
@@ -348,13 +337,10 @@ def tile_modulatemlp_pa_kernel(tc, x, w, weight, style_w, style_b, bias, out):
                 if step < GROUPS:
                     transpose_in(step, h)
                 for q in pair:
-                    if 0 <= step - 5 < GROUPS and q != SUMMED_TILE:
-                        rectify_out(step - 5, q)
+                    if 0 <= step - 5 < GROUPS:
+                        read_out(step - 5, q)
                     if 1 <= step - 3 < GROUPS:
                         demodulate(step - 3, q)
                         clamp(step - 3, q)
-                if 0 <= step - 5 < GROUPS:
-                    for t in pair:
-                        store(step - 5, t)
                 if h == 1 and 1 <= step - 3 < GROUPS:
                     rectify(step - 3)

@@ -24,7 +24,6 @@ BANK_ROWS = 2 * P
 BANK_SAMPLES = BANK_ROWS // POINTS
 GROUP_SAMPLES = GROUP // POINTS
 
-SUMMED_TILE = 3
 
 Y_BANKS = 3
 O_BANKS = 3
@@ -55,7 +54,7 @@ def quantise(nc, pool, grouped, name):
     nc.vector.quantize_mx(
         out=codes[:].bitcast(FP8X4),
         scales=scales[:],
-        in_=grouped[:].rearrange("p r t -> p (r t)"),
+        in_=grouped.rearrange("p r t -> p (r t)"),
     )
     return codes, scales
 
@@ -124,26 +123,35 @@ def tile_modulatemlp_pa_kernel(tc, x, w, weight, style_w, style_b, bias, out):
         for h, tag in enumerate(("o1", "o2")):
             sw_bank = psum.tile([P, HALVES, BANK_ROWS], F32, tag=tag)
             transpose_row_tiles(nc, sw_bank, sw_sb[:].bitcast(F32)[:, 2 * h : 2 * h + 2, :], ident)
-            nc.vector.tensor_copy(
+            copy = nc.vector.tensor_copy if h == 0 else nc.scalar.copy
+            copy(
                 out=sw_grp[:].bitcast(F32)[:, h * BANK_ROWS : (h + 1) * BANK_ROWS, :],
                 in_=sw_bank[:].rearrange("p u r -> p r u"),
             )
-        w_q = quantise(nc, const, w_grp, "w")
-        sw_q = quantise(nc, const, sw_grp, "sw")
+        w_q = quantise(nc, const, w_grp[:], "w")
+        sw_q = [
+            quantise(nc, const, sw_grp[:, h * BANK_ROWS : (h + 1) * BANK_ROWS, :], "sw%d" % h)
+            for h in range(HALVES)
+        ]
 
         wt_grp = const.tile([P, WIDTH, PACK], BF16, align_bytes=64)
         w2_grp = const.tile([P, WIDTH, PACK], BF16, align_bytes=64)
+        wt_banks = []
         for h, tag in enumerate(("y1", "y2")):
             wt_bank = psum.tile([P, HALVES, BANK_ROWS], F32, tag=tag)
             rows = slice(h * BANK_ROWS, (h + 1) * BANK_ROWS)
             transpose_row_tiles(nc, wt_bank, wt_sb[:].bitcast(F32)[:, 2 * h : 2 * h + 2, :], ident)
-            nc.scalar.activation(
-                out=w2_grp[:, rows, :].rearrange("p r (u e) -> p r u e", e=2),
-                in_=wt_bank[:].bitcast(BF16).rearrange("p u (r e) -> p r u e", e=2),
-                func=ACT.Square,
-            )
             nc.scalar.copy(
                 out=wt_grp[:].bitcast(F32)[:, rows, :], in_=wt_bank[:].rearrange("p u r -> p r u")
+            )
+            wt_banks.append(wt_bank)
+        for h, wt_bank in enumerate(wt_banks):
+            nc.scalar.activation(
+                out=w2_grp[:, h * BANK_ROWS : (h + 1) * BANK_ROWS, :].rearrange(
+                    "p r (u e) -> p r u e", e=2
+                ),
+                in_=wt_bank[:].bitcast(BF16).rearrange("p u (r e) -> p r u e", e=2),
+                func=ACT.Square,
             )
         nc.vector.tensor_copy(out=bias_rows[:CHUNKS, :], in_=bias_bf[:])
         vec_bank = psum.tile([P, 2, P], F32, tag="y0")
@@ -224,22 +232,14 @@ def tile_modulatemlp_pa_kernel(tc, x, w, weight, style_w, style_b, bias, out):
             )
 
         def rectify(g):
-            rest = fin.tile([P, CHUNKS, P], F32)
-            nc.gpsimd.tensor_scalar(
+            rest = mid.tile([P, CHUNKS, TILES // 2, P], F32)
+            nc.vector.tensor_scalar(
                 out=rest[:],
-                in0=low_tiles[g][:, :, SUMMED_TILE * P : (SUMMED_TILE + 1) * P],
-                scalar1=SLOPE * CLAMP,
-                scalar2=0.0,
-                op0=ALU.min,
-                op1=ALU.max,
-            )
-            nc.gpsimd.tensor_scalar(
-                out=rest[:],
-                in0=rest[:],
-                scalar1=1.0 / SLOPE - 1.0,
-                scalar2=0.0,
-                op0=ALU.mult,
-                op1=ALU.add,
+                in0=low_tiles[g][:].rearrange("p j (a b c) -> p j a b c", b=2, c=P)[:, :, :, 1, :],
+                scalar1=0.0,
+                scalar2=1.0 / SLOPE - 1.0,
+                op0=ALU.max,
+                op1=ALU.mult,
             )
             rest_tiles[g] = rest
 
@@ -248,13 +248,13 @@ def tile_modulatemlp_pa_kernel(tc, x, w, weight, style_w, style_b, bias, out):
             for j in range(CHUNKS):
                 columns = slice(j * P, (j + 1) * P)
                 low = low_tiles[g][:, j, t * P : (t + 1) * P]
-                if t == SUMMED_TILE:
+                if t % 2 == 1:
                     nc.tensor.matmul(
                         bank[:, columns], lhsT=low, rhs=ident[:], start=True, stop=False, is_transpose=True
                     )
                     nc.tensor.matmul(
                         bank[:, columns],
-                        lhsT=rest_tiles[g][:, j, :],
+                        lhsT=rest_tiles[g][:, j, t // 2, :],
                         rhs=ident[:],
                         start=False,
                         stop=True,
@@ -266,7 +266,7 @@ def tile_modulatemlp_pa_kernel(tc, x, w, weight, style_w, style_b, bias, out):
 
         def read_out(g, t):
             res = fin.tile([P, WIDTH], F32)
-            if t == SUMMED_TILE:
+            if t % 2 == 1:
                 nc.scalar.copy(out=res[:], in_=o_banks[g, t][:])
             else:
                 pos = fin.tile([P, WIDTH], F32)
@@ -282,9 +282,11 @@ def tile_modulatemlp_pa_kernel(tc, x, w, weight, style_w, style_b, bias, out):
         transpose_in(0, 0)
         transpose_in(0, 1)
 
+        wt_q = quantise(nc, const, wt_grp[:], "wt")
+
         style_ps = psum.tile([P, PACK, SAMPLES], F32, tag="y0")
         for t in range(PACK):
-            multiply_mx(nc, style_ps[:, t, :], sw_q, t * P, w_q)
+            multiply_mx(nc, style_ps[:, t, :], sw_q[t // 2], t % 2 * P, w_q)
         nc.vector.scalar_tensor_tensor(
             out=style4[:],
             in0=style_ps[:].rearrange("p t n -> p n t"),
@@ -297,11 +299,10 @@ def tile_modulatemlp_pa_kernel(tc, x, w, weight, style_w, style_b, bias, out):
         nc.scalar.activation(out=s2_grp[:], in_=style4[:], func=ACT.Square)
         modulate(0, 0)
         transpose_in(1, 0)
-        w2_q = quantise(nc, const, w2_grp, "w2")
-        s2_q = quantise(nc, const, s2_grp, "s2")
+        w2_q = quantise(nc, const, w2_grp[:], "w2")
+        s2_q = quantise(nc, const, s2_grp[:], "s2")
         modulate(0, 1)
-        wt_q = quantise(nc, const, wt_grp, "wt")
-        x_q[0] = quantise(nc, xq, grouped[0], "x")
+        x_q[0] = quantise(nc, xq, grouped[0][:], "x")
 
         d_ps = psum.tile([P, CHUNKS, SAMPLES], F32, tag="y1")
         for j in range(CHUNKS):
@@ -315,32 +316,27 @@ def tile_modulatemlp_pa_kernel(tc, x, w, weight, style_w, style_b, bias, out):
         )
 
         transpose_in(1, 1)
-        for j in range(CHUNKS):
-            multiply(0, j)
-            demodulate(0, j)
-            clamp(0, j)
-        rectify(0)
 
-        for step in range(2, GROUPS + 5):
+        for step in range(2, GROUPS + 4):
             if 1 <= step - 2 < GROUPS:
-                x_q[step - 2] = quantise(nc, xq, grouped[step - 2], "x")
+                x_q[step - 2] = quantise(nc, xq, grouped[step - 2][:], "x")
             for h in range(2):
                 pair = (2 * h, 2 * h + 1)
-                if 0 <= step - 5 < GROUPS:
+                if 0 <= step - 4 < GROUPS:
                     for t in pair:
-                        transpose_out(step - 5, t)
-                if 1 <= step - 3 < GROUPS:
+                        transpose_out(step - 4, t)
+                if 0 <= step - 2 < GROUPS:
                     for j in pair:
-                        multiply(step - 3, j)
+                        multiply(step - 2, j)
                 if step - 1 < GROUPS:
                     modulate(step - 1, h)
                 if step < GROUPS:
                     transpose_in(step, h)
                 for q in pair:
-                    if 0 <= step - 5 < GROUPS:
-                        read_out(step - 5, q)
-                    if 1 <= step - 3 < GROUPS:
-                        demodulate(step - 3, q)
-                        clamp(step - 3, q)
-                if h == 1 and 1 <= step - 3 < GROUPS:
+                    if 0 <= step - 4 < GROUPS:
+                        read_out(step - 4, q)
+                    if 0 <= step - 2 < GROUPS:
+                        demodulate(step - 2, q)
+                        clamp(step - 2, q)
+                if h == 0 and 0 <= step - 3 < GROUPS:
                     rectify(step - 3)

@@ -26,6 +26,7 @@ GROUP_SAMPLES = GROUP // POINTS
 
 
 Y_BANKS = 3
+LOADS_AHEAD = 4
 O_BANKS = 3
 
 EPS = 1e-8
@@ -78,7 +79,7 @@ def tile_modulatemlp_pa_kernel(tc, x, w, weight, style_w, style_b, bias, out):
     out_rows = out.rearrange("n l o -> (n l) o")
 
     with tc.tile_pool(name="const", bufs=1) as const, tc.tile_pool(
-        name="xin", bufs=GROUPS
+        name="xin", bufs=LOADS_AHEAD + 3
     ) as xin, tc.tile_pool(name="xq", bufs=3) as xq, tc.tile_pool(
         name="mid", bufs=5
     ) as mid, tc.tile_pool(name="fin", bufs=6) as fin, tc.psum_pool(name="psum", bufs=1) as psum, tc.manual_schedule():
@@ -105,14 +106,18 @@ def tile_modulatemlp_pa_kernel(tc, x, w, weight, style_w, style_b, bias, out):
             in_=style_b.rearrange("(u q) -> u q", u=HALVES),
         )
         nc.sync.dma_start(out=bias_bf[:], in_=bias.rearrange("(j p) -> j p", p=P))
-        x_tiles = []
-        for g in range(GROUPS):
+        x_tiles = {}
+
+        def load(g):
             x_sb = xin.tile([P, TILES, WIDTH], BF16)
             nc.sync.dma_start(
                 out=x_sb[:],
                 in_=x_rows[g * GROUP : (g + 1) * GROUP, :].rearrange("(t p) c -> p t c", p=P),
             )
-            x_tiles.append(x_sb)
+            x_tiles[g] = x_sb
+
+        for g in range(2 + LOADS_AHEAD):
+            load(g)
 
         w_bank = psum.tile([P, HALVES, P], F32, tag="o0")
         transpose_row_tiles(nc, w_bank, w_sb[:].bitcast(F32), ident)
@@ -220,8 +225,8 @@ def tile_modulatemlp_pa_kernel(tc, x, w, weight, style_w, style_b, bias, out):
                     bias=bias_g[:, j : j + 1],
                 )
 
-        def clamp(g, j):
-            part = low_tiles[g][:, j, :]
+        def clamp(g, h):
+            part = low_tiles[g][:, 2 * h : 2 * h + 2, :]
             nc.gpsimd.tensor_scalar(
                 out=part,
                 in0=part,
@@ -318,6 +323,8 @@ def tile_modulatemlp_pa_kernel(tc, x, w, weight, style_w, style_b, bias, out):
         transpose_in(1, 1)
 
         for step in range(2, GROUPS + 4):
+            if step + LOADS_AHEAD < GROUPS:
+                load(step + LOADS_AHEAD)
             if 1 <= step - 2 < GROUPS:
                 x_q[step - 2] = quantise(nc, xq, grouped[step - 2][:], "x")
             for h in range(2):
@@ -332,11 +339,12 @@ def tile_modulatemlp_pa_kernel(tc, x, w, weight, style_w, style_b, bias, out):
                     modulate(step - 1, h)
                 if step < GROUPS:
                     transpose_in(step, h)
+                if h == 1 and 0 <= step - 3 < GROUPS:
+                    rectify(step - 3)
                 for q in pair:
                     if 0 <= step - 4 < GROUPS:
                         read_out(step - 4, q)
                     if 0 <= step - 2 < GROUPS:
                         demodulate(step - 2, q)
-                        clamp(step - 2, q)
-                if h == 0 and 0 <= step - 3 < GROUPS:
-                    rectify(step - 3)
+                if 0 <= step - 2 < GROUPS:
+                    clamp(step - 2, h)

import math

import concourse.mybir as mybir
from concourse.masks import make_identity

F32 = mybir.dt.float32
BF16 = mybir.dt.bfloat16
U32 = mybir.dt.uint32
U8 = mybir.dt.uint8
FP8X4 = mybir.dt.float8_e4m3fn_x4
ALU = mybir.AluOpType
ACT = mybir.ActivationFunctionType

P = 128
PACK = 4
HALVES = 2
SAMPLES, POINTS, WIDTH = 128, 64, 512
CHUNKS = WIDTH // P
TOKENS = SAMPLES * POINTS
GROUP = 512
GROUPS = TOKENS // GROUP
TILES = GROUP // P
BANK_ROWS = 2 * P
BANK_SAMPLES = BANK_ROWS // POINTS
GROUP_SAMPLES = GROUP // POINTS


Y_BANKS = 3
LOADS_AHEAD = 4
O_BANKS = 3

EPS = 1e-8
CLAMP = 256.0
SLOPE = 0.2
GAIN = math.sqrt(2.0)
LOW_GAIN = GAIN * SLOPE
LOW_GAIN_SQUARED = 2.0 * SLOPE * SLOPE
STYLE_WSCALE = 1.0 / math.sqrt(WIDTH)

FLOPS = 2 * TOKENS * WIDTH * WIDTH + 2 * 2 * SAMPLES * WIDTH * WIDTH


def transpose_row_tiles(nc, bank, words, ident):
    for s in range(words.shape[1]):
        for u in range(HALVES):
            nc.tensor.transpose(
                bank[:, u, s * P : (s + 1) * P], words[:, s, u * P : (u + 1) * P], ident[:]
            )


def quantise(nc, pool, grouped, name):
    columns = grouped.shape[1]
    codes = pool.tile([P, columns], U32, align_bytes=64, name=name + "_codes")
    scales = pool.tile([P, columns], U8, align_bytes=64, name=name + "_scales")
    nc.vector.quantize_mx(
        out=codes[:].bitcast(FP8X4),
        scales=scales[:],
        in_=grouped.rearrange("p r t -> p (r t)"),
    )
    return codes, scales


def multiply_mx(nc, acc, stationary, first_column, moving):
    cols = slice(first_column, first_column + P)
    nc.tensor.matmul_mx(
        out=acc,
        lhsT=stationary[0][:, cols].bitcast(FP8X4),
        lhsT_scale=stationary[1][:, cols],
        rhs=moving[0][:].bitcast(FP8X4),
        rhs_scale=moving[1][:],
        start=True,
        stop=True,
    )


def tile_modulatemlp_pa_kernel(tc, x, w, weight, style_w, style_b, bias, out):
    nc = tc.nc
    x_rows = x.rearrange("n l c -> (n l) c")
    out_rows = out.rearrange("n l o -> (n l) o")

    with tc.tile_pool(name="const", bufs=1) as const, tc.tile_pool(
        name="xin", bufs=LOADS_AHEAD + 3
    ) as xin, tc.tile_pool(name="xq", bufs=3) as xq, tc.tile_pool(
        name="mid", bufs=5
    ) as mid, tc.tile_pool(name="fin", bufs=6) as fin, tc.psum_pool(name="psum", bufs=1) as psum, tc.manual_schedule():
        ident = const.tile([P, P], F32)
        make_identity(nc, ident[:])

        style_b_rows = const.tile([P, P], F32)
        nc.vector.memset(style_b_rows[:], 0.0)
        bias_rows = const.tile([P, P], F32)
        nc.vector.memset(bias_rows[:], 0.0)
        bias_bf = const.tile([CHUNKS, P], BF16)
        w_sb = const.tile([P, 1, WIDTH], BF16)
        nc.sync.dma_start(out=w_sb[:, 0, :], in_=w)
        sw_sb = const.tile([P, PACK, WIDTH], BF16)
        sw_halves = style_w.rearrange("(u p e) k -> u p (e k)", u=HALVES, e=2)
        for u in range(HALVES):
            nc.sync.dma_start(
                out=sw_sb[:, 2 * u : 2 * u + 2, :].rearrange("p e k -> p (e k)"), in_=sw_halves[u]
            )
        wt_sb = const.tile([P, CHUNKS, WIDTH], BF16)
        nc.sync.dma_start(out=wt_sb[:], in_=weight.rearrange("(j p) c -> p j c", p=P))
        nc.sync.dma_start(
            out=style_b_rows[:HALVES, :].bitcast(BF16),
            in_=style_b.rearrange("(u q) -> u q", u=HALVES),
        )
        nc.sync.dma_start(out=bias_bf[:], in_=bias.rearrange("(j p) -> j p", p=P))
        x_tiles = {}

        def load(g):
            x_sb = xin.tile([P, TILES, WIDTH], BF16)
            nc.sync.dma_start(
                out=x_sb[:],
                in_=x_rows[g * GROUP : (g + 1) * GROUP, :].rearrange("(t p) c -> p t c", p=P),
            )
            x_tiles[g] = x_sb

        for g in range(2 + LOADS_AHEAD):
            load(g)

        w_bank = psum.tile([P, HALVES, P], F32, tag="o0")
        transpose_row_tiles(nc, w_bank, w_sb[:].bitcast(F32), ident)
        w_grp = const.tile([P, SAMPLES, PACK], BF16, align_bytes=64)
        nc.vector.tensor_copy(out=w_grp[:].bitcast(F32), in_=w_bank[:].rearrange("p u r -> p r u"))

        sw_grp = const.tile([P, WIDTH, PACK], BF16, align_bytes=64)
        for h, tag in enumerate(("o1", "o2")):
            sw_bank = psum.tile([P, HALVES, BANK_ROWS], F32, tag=tag)
            transpose_row_tiles(nc, sw_bank, sw_sb[:].bitcast(F32)[:, 2 * h : 2 * h + 2, :], ident)
            copy = nc.vector.tensor_copy if h == 0 else nc.scalar.copy
            copy(
                out=sw_grp[:].bitcast(F32)[:, h * BANK_ROWS : (h + 1) * BANK_ROWS, :],
                in_=sw_bank[:].rearrange("p u r -> p r u"),
            )
        w_q = quantise(nc, const, w_grp[:], "w")
        sw_q = [
            quantise(nc, const, sw_grp[:, h * BANK_ROWS : (h + 1) * BANK_ROWS, :], "sw%d" % h)
            for h in range(HALVES)
        ]

        wt_grp = const.tile([P, WIDTH, PACK], BF16, align_bytes=64)
        w2_grp = const.tile([P, WIDTH, PACK], BF16, align_bytes=64)
        wt_banks = []
        for h, tag in enumerate(("y1", "y2")):
            wt_bank = psum.tile([P, HALVES, BANK_ROWS], F32, tag=tag)
            rows = slice(h * BANK_ROWS, (h + 1) * BANK_ROWS)
            transpose_row_tiles(nc, wt_bank, wt_sb[:].bitcast(F32)[:, 2 * h : 2 * h + 2, :], ident)
            nc.scalar.copy(
                out=wt_grp[:].bitcast(F32)[:, rows, :], in_=wt_bank[:].rearrange("p u r -> p r u")
            )
            wt_banks.append(wt_bank)
        for h, wt_bank in enumerate(wt_banks):
            nc.scalar.activation(
                out=w2_grp[:, h * BANK_ROWS : (h + 1) * BANK_ROWS, :].rearrange(
                    "p r (u e) -> p r u e", e=2
                ),
                in_=wt_bank[:].bitcast(BF16).rearrange("p u (r e) -> p r u e", e=2),
                func=ACT.Square,
            )
        nc.vector.tensor_copy(out=bias_rows[:CHUNKS, :], in_=bias_bf[:])
        vec_bank = psum.tile([P, 2, P], F32, tag="y0")
        nc.tensor.transpose(vec_bank[:, 0, :], style_b_rows[:], ident[:])
        nc.tensor.transpose(vec_bank[:, 1, :], bias_rows[:], ident[:])
        style_b_words = const.tile([P, HALVES], F32)
        nc.vector.tensor_copy(out=style_b_words[:], in_=vec_bank[:, 0, :HALVES])
        bias_g = const.tile([P, CHUNKS], F32)
        nc.vector.tensor_scalar(
            out=bias_g[:], in0=vec_bank[:, 1, :CHUNKS], scalar1=LOW_GAIN, scalar2=None, op0=ALU.mult
        )

        style4 = const.tile([P, SAMPLES, PACK], F32)
        demod = const.tile([P, CHUNKS, SAMPLES], F32)
        x_banks = {}
        grouped = {}
        x_q = {}
        y_banks = {}
        low_tiles = {}
        rest_tiles = {}
        o_banks = {}

        def transpose_in(g, h):
            bank = psum.tile([P, HALVES, BANK_ROWS], F32, tag="xT%d" % h)
            transpose_row_tiles(
                nc, bank, x_tiles[g][:].bitcast(F32)[:, 2 * h : 2 * h + 2, :], ident
            )
            x_banks[g, h] = bank

        def modulate(g, h):
            if h == 0:
                x_grp = xq.tile([P, GROUP, PACK], BF16, align_bytes=64)
                grouped[g] = x_grp
            first = g * GROUP_SAMPLES + h * BANK_SAMPLES
            nc.vector.tensor_tensor(
                out=grouped[g][:, h * BANK_ROWS : (h + 1) * BANK_ROWS, :].rearrange(
                    "p (n l) (u e) -> p n l u e", l=POINTS, e=2
                ),
                in0=x_banks[g, h][:]
                .bitcast(BF16)
                .rearrange("p u (n l e) -> p n l u e", l=POINTS, e=2),
                in1=style4[:, first : first + BANK_SAMPLES, :]
                .rearrange("p n (u e) -> p n u e", e=2)
                .unsqueeze(2)
                .to_broadcast([P, BANK_SAMPLES, POINTS, HALVES, 2]),
                op=ALU.mult,
            )

        def multiply(g, j):
            y = psum.tile([P, GROUP], F32, tag="y%d" % ((g * CHUNKS + j) % Y_BANKS))
            multiply_mx(nc, y[:], wt_q, j * P, x_q[g])
            y_banks[g, j] = y

        def demodulate(g, j):
            if j == 0:
                low = mid.tile([P, CHUNKS, GROUP], F32)
                low_tiles[g] = low
            for s in range(GROUP_SAMPLES):
                n = g * GROUP_SAMPLES + s
                cols = slice(s * POINTS, (s + 1) * POINTS)
                nc.scalar.activation(
                    out=low_tiles[g][:, j, cols],
                    in_=y_banks[g, j][:, cols],
                    func=ACT.Identity,
                    scale=demod[:, j, n : n + 1],
                    bias=bias_g[:, j : j + 1],
                )

        def clamp(g, h):
            part = low_tiles[g][:, 2 * h : 2 * h + 2, :]
            nc.gpsimd.tensor_scalar(
                out=part,
                in0=part,
                scalar1=SLOPE * CLAMP,
                scalar2=-CLAMP,
                op0=ALU.min,
                op1=ALU.max,
            )

        def rectify(g):
            rest = mid.tile([P, CHUNKS, TILES // 2, P], F32)
            nc.vector.tensor_scalar(
                out=rest[:],
                in0=low_tiles[g][:].rearrange("p j (a b c) -> p j a b c", b=2, c=P)[:, :, :, 1, :],
                scalar1=0.0,
                scalar2=1.0 / SLOPE - 1.0,
                op0=ALU.max,
                op1=ALU.mult,
            )
            rest_tiles[g] = rest

        def transpose_out(g, t):
            bank = psum.tile([P, WIDTH], F32, tag="o%d" % ((g * TILES + t) % O_BANKS))
            for j in range(CHUNKS):
                columns = slice(j * P, (j + 1) * P)
                low = low_tiles[g][:, j, t * P : (t + 1) * P]
                if t % 2 == 1:
                    nc.tensor.matmul(
                        bank[:, columns], lhsT=low, rhs=ident[:], start=True, stop=False, is_transpose=True
                    )
                    nc.tensor.matmul(
                        bank[:, columns],
                        lhsT=rest_tiles[g][:, j, t // 2, :],
                        rhs=ident[:],
                        start=False,
                        stop=True,
                        is_transpose=True,
                    )
                else:
                    nc.tensor.transpose(bank[:, columns], low, ident[:])
            o_banks[g, t] = bank

        def read_out(g, t):
            res = fin.tile([P, WIDTH], F32)
            if t % 2 == 1:
                nc.scalar.copy(out=res[:], in_=o_banks[g, t][:])
            else:
                pos = fin.tile([P, WIDTH], F32)
                nc.scalar.activation(
                    out=pos[:], in_=o_banks[g, t][:], func=ACT.Relu, scale=1.0 / SLOPE - 1.0
                )
                nc.vector.tensor_tensor(
                    out=res[:], in0=o_banks[g, t][:], in1=pos[:], op=ALU.add
                )
            first = g * GROUP + t * P
            nc.sync.dma_start(out=out_rows[first : first + P, :], in_=res[:])

        transpose_in(0, 0)
        transpose_in(0, 1)

        wt_q = quantise(nc, const, wt_grp[:], "wt")

        style_ps = psum.tile([P, PACK, SAMPLES], F32, tag="y0")
        for t in range(PACK):
            multiply_mx(nc, style_ps[:, t, :], sw_q[t // 2], t % 2 * P, w_q)
        nc.vector.scalar_tensor_tensor(
            out=style4[:],
            in0=style_ps[:].rearrange("p t n -> p n t"),
            scalar=STYLE_WSCALE,
            in1=style_b_words[:].bitcast(BF16).unsqueeze(1).to_broadcast([P, SAMPLES, PACK]),
            op0=ALU.mult,
            op1=ALU.add,
        )
        s2_grp = const.tile([P, SAMPLES, PACK], BF16, align_bytes=64)
        nc.scalar.activation(out=s2_grp[:], in_=style4[:], func=ACT.Square)
        modulate(0, 0)
        transpose_in(1, 0)
        w2_q = quantise(nc, const, w2_grp[:], "w2")
        s2_q = quantise(nc, const, s2_grp[:], "s2")
        modulate(0, 1)
        x_q[0] = quantise(nc, xq, grouped[0][:], "x")

        d_ps = psum.tile([P, CHUNKS, SAMPLES], F32, tag="y1")
        for j in range(CHUNKS):
            multiply_mx(nc, d_ps[:, j, :], w2_q, j * P, s2_q)
        nc.scalar.activation(
            out=demod[:],
            in_=d_ps[:],
            func=ACT.Abs_reciprocal_sqrt,
            scale=1.0 / LOW_GAIN_SQUARED,
            bias=EPS / LOW_GAIN_SQUARED,
        )

        transpose_in(1, 1)

        for step in range(2, GROUPS + 4):
            if step + LOADS_AHEAD < GROUPS:
                load(step + LOADS_AHEAD)
            if 1 <= step - 2 < GROUPS:
                x_q[step - 2] = quantise(nc, xq, grouped[step - 2][:], "x")
            for h in range(2):
                pair = (2 * h, 2 * h + 1)
                if 0 <= step - 4 < GROUPS:
                    for t in pair:
                        transpose_out(step - 4, t)
                if 0 <= step - 2 < GROUPS:
                    for j in pair:
                        multiply(step - 2, j)
                if step - 1 < GROUPS:
                    modulate(step - 1, h)
                if step < GROUPS:
                    transpose_in(step, h)
                if h == 1 and 0 <= step - 3 < GROUPS:
                    rectify(step - 3)
                for q in pair:
                    if 0 <= step - 4 < GROUPS:
                        read_out(step - 4, q)
                    if 0 <= step - 2 < GROUPS:
                        demodulate(step - 2, q)
                if 0 <= step - 2 < GROUPS:
                    clamp(step - 2, h)
